import numpy as np
import ml_dtypes


def mxq(x, axis, fmt="e4m3"):
    dtype, down = {"e4m3": (ml_dtypes.float8_e4m3fn, 7), "e5m2": (ml_dtypes.float8_e5m2, 14)}[fmt]
    v = np.moveaxis(np.asarray(x, np.float32).astype(ml_dtypes.bfloat16).astype(np.float64), axis, -1)
    blocks = v.reshape(v.shape[:-1] + (-1, 32))
    amax = np.abs(blocks).max(-1, keepdims=True)
    byte = np.maximum(np.where(amax > 0, np.frexp(amax)[1] - 1 + 127, 0) - down, 1)
    scale = np.exp2(byte - 127.0)
    codes = (blocks / scale).astype(np.float32).astype(dtype).astype(np.float64)
    return np.moveaxis((codes * scale).reshape(v.shape), -1, axis)


WIDE = False


def mx_kscale(k):
    if not WIDE:
        return np.ones(k)
    levels = np.array([10, -10, 5, -5, 0])
    if k % 512:
        return np.exp2(np.random.permutation(np.resize(levels, k // 32))).repeat(32)
    a = np.empty((k // 512, 16))
    for p in range(k // 512):
        a[p, :8] = np.random.permutation(np.resize(levels, 8))
        for g in range(8):
            far = levels[np.abs(levels - a[p, g]) >= 10]
            a[p, g + 8] = far[np.random.randint(len(far))]
    return np.exp2(a.ravel()).repeat(32)


BF16 = ml_dtypes.bfloat16


def bf(x):
    return np.asarray(x, np.float32).astype(BF16)


def f64(x):
    return np.asarray(x).astype(np.float64)


B, S, H, F = 512, 8, 512, 512


def setup_inputs():
    s = mx_kscale(H)
    t = mx_kscale(F)
    s2 = np.concatenate([s, s])
    return {"h": bf(np.random.standard_normal((B, S, H)) * s),
            "ew1": bf(np.random.standard_normal((2 * H, F)) / np.sqrt(2 * H) / s2[:, None] * t),
            "eb1": bf(np.random.standard_normal(F) * 0.3 * t),
            "ew2": bf(np.random.standard_normal((F, H)) / np.sqrt(F) / t[:, None]),
            "eb2": bf(np.random.standard_normal(H) * 0.3)}


def edge_mlp(xq, w1q, b1, w2q, b2):
    hid = np.maximum((xq @ w1q) + b1, 0.0)
    return (mxq(hid, 2, "e4m3") @ w2q) + b2


def reference(h, ew1, eb1, ew2, eb2):
    hq = mxq(f64(h), 2, "e4m3")
    w1q = mxq(f64(ew1), 0, "e4m3")
    w2q = mxq(f64(ew2), 0, "e4m3")
    b1, b2 = f64(eb1), f64(eb2)
    left = hq[:, :-1, :]
    right = hq[:, 1:, :]
    m_lr = edge_mlp(np.concatenate([left, right], axis=-1), w1q, b1, w2q, b2)
    m_rl = edge_mlp(np.concatenate([right, left], axis=-1), w1q, b1, w2q, b2)
    zcol = np.zeros_like(m_lr[:, :1, :])
    return np.concatenate([zcol, m_lr], axis=1) + np.concatenate([m_rl, zcol], axis=1)

@@ -1,0 +1,246 @@
+from contextlib import ExitStack
+
+import concourse.mybir as mybir
+from concourse.masks import make_identity
+
+BF16 = mybir.dt.bfloat16
+F32 = mybir.dt.float32
+U32 = mybir.dt.uint32
+U8 = mybir.dt.uint8
+FP8X4 = mybir.dt.float8_e4m3fn_x4
+RELU = mybir.ActivationFunctionType.Relu
+IDENTITY = mybir.ActivationFunctionType.Identity
+ADD = mybir.AluOpType.add
+MULT = mybir.AluOpType.mult
+
+P = 128
+PACK = 4
+CHAINS, NODES, WIDTH = 512, 8, 512
+EDGES = NODES - 1
+CHUNKS = WIDTH // P
+WORDS = WIDTH // 2
+HALVES = 2
+HALF = CHAINS // HALVES
+HALF_TILES = HALF // P
+LR, RL = 0, 1
+LAG = 2
+
+FLOPS = 2 * 2 * CHAINS * EDGES * (2 * WIDTH * WIDTH + WIDTH * WIDTH)
+
+
+def tile_graphnetlayer_pa_t_kernel(tc, h, ew1, eb1, ew2, eb2, out):
+    nc = tc.nc
+    with ExitStack() as stack:
+        stack.enter_context(tc.manual_schedule())
+        consts = stack.enter_context(tc.tile_pool(name="consts", bufs=1))
+        weights = stack.enter_context(tc.tile_pool(name="weights", bufs=1))
+        nodes = stack.enter_context(tc.tile_pool(name="nodes", bufs=1))
+        h_raw_pool = stack.enter_context(tc.tile_pool(name="h_raw_pool", bufs=HALVES * NODES // 2))
+        h_grouped_pool = stack.enter_context(tc.tile_pool(name="h_grouped_pool", bufs=4))
+        planes_pool = stack.enter_context(tc.tile_pool(name="planes_pool", bufs=2))
+        hid_grouped_pool = stack.enter_context(tc.tile_pool(name="hid_grouped_pool", bufs=2))
+        hid_pool = stack.enter_context(tc.tile_pool(name="hid_pool", bufs=6))
+        result_pool = stack.enter_context(tc.tile_pool(name="result_pool", bufs=6))
+        acc1_pool = stack.enter_context(tc.psum_pool(name="acc1_pool", bufs=4))
+        aux_pool = stack.enter_context(tc.psum_pool(name="aux_pool", bufs=4))
+
+        b1_bf16 = consts.tile([P, CHUNKS], BF16)
+        nc.scalar.dma_start(out=b1_bf16[:], in_=eb1.rearrange("(p c) -> p c", c=CHUNKS))
+        b1 = consts.tile([P, CHUNKS], F32)
+        ones = consts.tile([P, P], BF16)
+        nc.vector.memset(ones[:], 1.0)
+        b2_rows = consts.tile([P, WIDTH], BF16)
+        nc.vector.memset(b2_rows[:], 0.0)
+        nc.scalar.dma_start(out=b2_rows[0:1, :], in_=eb2.rearrange("(o n) -> o n", o=1))
+        nc.scalar.activation(out=b1[:], in_=b1_bf16[:], func=IDENTITY)
+        b2_once = consts.tile([P, WIDTH], F32)
+        b2_twice = consts.tile([P, WIDTH], F32)
+
+        def spread_b2():
+            b2_spread = aux_pool.tile([P, WIDTH], F32, tag="aux")
+            nc.tensor.matmul(out=b2_spread[:], lhsT=ones[:], rhs=b2_rows[:], start=True, stop=True)
+            nc.vector.tensor_copy(out=b2_once[:], in_=b2_spread[:])
+            nc.vector.tensor_scalar(out=b2_twice[:], in0=b2_spread[:], scalar1=2.0, scalar2=None, op0=MULT)
+
+        w1_raw = weights.tile([P, 2, PACK, WIDTH], BF16)
+        for a in range(2):
+            nc.sync.dma_start(
+                out=w1_raw[:, a, :, :],
+                in_=ew1[a * WIDTH : (a + 1) * WIDTH, :].rearrange("(q t) f -> q t f", t=PACK),
+            )
+
+        h_raw = {}
+
+        def load_node_pair(g):
+            for half in range(HALVES):
+                raw = h_raw_pool.tile([P, HALF_TILES * 2 * WIDTH], BF16, name="h_raw", tag="h_raw")
+                nc.sync.dma_start(
+                    out=raw[:].rearrange("p (t s k) -> p t s k", t=HALF_TILES, s=2),
+                    in_=h[half * HALF : (half + 1) * HALF, 2 * g : 2 * g + 2, :].rearrange("(t p) s k -> p t s k", p=P),
+                )
+                h_raw[(g, half)] = raw
+
+        load_node_pair(0)
+        w2_raw = weights.tile([P, PACK, WIDTH], BF16)
+        nc.sync.dma_start(out=w2_raw[:], in_=ew2.rearrange("(p t) n -> p t n", t=PACK))
+        for g in range(1, NODES // 2):
+            load_node_pair(g)
+
+        ident = consts.tile([P, P], F32)
+        make_identity(nc, ident[:])
+
+        w1_grouped = weights.tile([P, 2, CHUNKS, P, PACK], BF16, align_bytes=64)
+        w1_codes = weights.tile([P, 2, WIDTH], U32, align_bytes=64)
+        w1_scales = weights.tile([P, 2, WIDTH], U8, align_bytes=64)
+        for a in range(2):
+            nc.vector.tensor_copy(
+                out=w1_grouped[:, a, :, :, :],
+                in_=w1_raw[:, a, :, :].rearrange("q t (m c) -> q c m t", c=CHUNKS),
+            )
+        for a in range(2):
+            nc.vector.quantize_mx(
+                out=w1_codes[:, a, :].bitcast(FP8X4),
+                scales=w1_scales[:, a, :],
+                in_=w1_grouped[:, a, :, :, :].rearrange("q c m t -> q (c m t)"),
+            )
+
+        w2_grouped = weights.tile([P, WIDTH, PACK], BF16, align_bytes=64)
+        w2_codes = weights.tile([P, WIDTH], U32, align_bytes=64)
+        w2_scales = weights.tile([P, WIDTH], U8, align_bytes=64)
+
+        def regroup(grouped, planes):
+            nc.vector.tensor_copy(
+                out=grouped[:].rearrange("p (c i) t -> p c t i", i=4),
+                in_=planes[:].rearrange("p t (c i) -> p c t i", i=4),
+            )
+
+        h_codes = nodes.tile([P, NODES, CHAINS], U32, align_bytes=64)
+        h_scales = nodes.tile([P, NODES, CHAINS], U8, align_bytes=64)
+        h_grouped = {}
+
+        def transpose_node(s, half):
+            words = h_raw[(s // 2, half)][:].bitcast(F32)
+            bank = aux_pool.tile([P, 2, HALF], F32, tag="aux")
+            for u in range(2):
+                for t in range(HALF_TILES):
+                    first = (2 * t + s % 2) * WORDS
+                    nc.tensor.transpose(
+                        bank[:, u, t * P : (t + 1) * P], words[:, first + u : first + WORDS : 2], ident[:]
+                    )
+            grouped = h_grouped_pool.tile([P, HALF * PACK], BF16, name="h_grouped", tag="h_grouped", align_bytes=64)
+            nc.scalar.copy(
+                out=grouped[:].bitcast(F32).rearrange("p (c u) -> p c u", u=2),
+                in_=bank[:].rearrange("p u c -> p c u"),
+            )
+            h_grouped[(s, half)] = grouped
+
+        def quantise_node(s, half):
+            chains = slice(half * HALF, (half + 1) * HALF)
+            nc.vector.quantize_mx(
+                out=h_codes[:, s, chains].bitcast(FP8X4), scales=h_scales[:, s, chains], in_=h_grouped[(s, half)][:]
+            )
+
+        planes = {}
+        hid_grouped = {}
+        hid_codes = {}
+        hid_scales = {}
+
+        def layer1(i, half):
+            chains = slice(half * HALF, (half + 1) * HALF)
+            hidden = planes_pool.tile([P, CHUNKS, 2, HALF], BF16, name="planes", tag="planes")
+            for c in range(CHUNKS):
+                acc1 = acc1_pool.tile([P, 2, HALF], F32)
+                for direction, joined in ((LR, (i, i + 1)), (RL, (i + 1, i))):
+                    for a in range(2):
+                        nc.tensor.matmul_mx(
+                            out=acc1[:, direction, :],
+                            lhsT=w1_codes[:, a, c * P : (c + 1) * P].bitcast(FP8X4),
+                            lhsT_scale=w1_scales[:, a, c * P : (c + 1) * P],
+                            rhs=h_codes[:, joined[a], chains].bitcast(FP8X4),
+                            rhs_scale=h_scales[:, joined[a], chains],
+                            start=(a == 0),
+                            stop=(a == 1),
+                        )
+                nc.scalar.activation(
+                    out=hidden[:, c, :, :], in_=acc1[:], func=RELU, bias=b1[:, c : c + 1], scale=1.0
+                )
+            planes[(i, half)] = hidden
+
+        def regroup_hidden(i, half):
+            grouped = hid_grouped_pool.tile([P, 2 * HALF, PACK], BF16, name="hid_grouped", tag="hid_grouped", align_bytes=64)
+            regroup(grouped, planes[(i, half)][:].rearrange("p t d w -> p t (d w)"))
+            hid_grouped[(i, half)] = grouped
+
+        def quantise_hidden(i, half):
+            codes = hid_pool.tile([P, 2 * HALF], U32, name="hid_codes", tag="hid_codes", align_bytes=64)
+            scales = hid_pool.tile([P, 2 * HALF], U8, name="hid_scales", tag="hid_scales", align_bytes=64)
+            nc.vector.quantize_mx(
+                out=codes[:].bitcast(FP8X4),
+                scales=scales[:],
+                in_=hid_grouped[(i, half)][:].rearrange("p w t -> p (w t)"),
+            )
+            hid_codes[(i, half)] = codes
+            hid_scales[(i, half)] = scales
+
+        def layer2(j, half):
+            messages = []
+            if j > 0:
+                messages.append((j - 1, LR))
+            if j < EDGES:
+                messages.append((j, RL))
+            bias = b2_twice if len(messages) == 2 else b2_once
+            for t in range(HALF_TILES):
+                acc2 = aux_pool.tile([P, WIDTH], F32, tag="aux")
+                for n, (i, direction) in enumerate(messages):
+                    columns = slice(direction * HALF + t * P, direction * HALF + (t + 1) * P)
+                    nc.tensor.matmul_mx(
+                        out=acc2[:],
+                        lhsT=hid_codes[(i, half)][:, columns].bitcast(FP8X4),
+                        lhsT_scale=hid_scales[(i, half)][:, columns],
+                        rhs=w2_codes[:].bitcast(FP8X4),
+                        rhs_scale=w2_scales[:],
+                        start=(n == 0),
+                        stop=(n == len(messages) - 1),
+                    )
+                result = result_pool.tile([P, WIDTH], F32)
+                nc.vector.tensor_tensor(out=result[:], in0=acc2[:], in1=bias[:], op=ADD)
+                first_chain = half * HALF + t * P
+                nc.sync.dma_start(out=out[first_chain : first_chain + P, j, :], in_=result[:])
+
+        for half in range(HALVES):
+            for s in range(2):
+                transpose_node(s, half)
+        for half in range(HALVES):
+            for s in range(2):
+                quantise_node(s, half)
+        regroup(w2_grouped, w2_raw)
+
+        def second_layer_after(unit):
+            i, half = unit
+            layer2(i, half)
+            if i == EDGES - 1:
+                layer2(NODES - 1, half)
+
+        units = [(i, half) for i in range(EDGES) for half in range(HALVES)]
+        for u, (i, half) in enumerate(units):
+            layer1(i, half)
+            if u == 0:
+                spread_b2()
+                nc.vector.quantize_mx(
+                    out=w2_codes[:].bitcast(FP8X4),
+                    scales=w2_scales[:],
+                    in_=w2_grouped[:].rearrange("p w t -> p (w t)"),
+                )
+            if u >= LAG:
+                second_layer_after(units[u - LAG])
+            new_node = half == 0 and i + 2 < NODES
+            if new_node:
+                for other in range(HALVES):
+                    transpose_node(i + 2, other)
+            regroup_hidden(i, half)
+            if new_node:
+                for other in range(HALVES):
+                    quantise_node(i + 2, other)
+            quantise_hidden(i, half)
+        for unit in units[len(units) - LAG :]:
+            second_layer_after(unit)

@@ -23,7 +23,6 @@ HALVES = 2
 HALF = CHAINS // HALVES
 HALF_TILES = HALF // P
 LR, RL = 0, 1
-LAG = 2
 
 FLOPS = 2 * 2 * CHAINS * EDGES * (2 * WIDTH * WIDTH + WIDTH * WIDTH)
 
@@ -31,7 +30,6 @@ FLOPS = 2 * 2 * CHAINS * EDGES * (2 * WIDTH * WIDTH + WIDTH * WIDTH)
 def tile_graphnetlayer_pa_t_kernel(tc, h, ew1, eb1, ew2, eb2, out):
     nc = tc.nc
     with ExitStack() as stack:
-        stack.enter_context(tc.manual_schedule())
         consts = stack.enter_context(tc.tile_pool(name="consts", bufs=1))
         weights = stack.enter_context(tc.tile_pool(name="weights", bufs=1))
         nodes = stack.enter_context(tc.tile_pool(name="nodes", bufs=1))
@@ -41,189 +39,224 @@ def tile_graphnetlayer_pa_t_kernel(tc, h, ew1, eb1, ew2, eb2, out):
         hid_grouped_pool = stack.enter_context(tc.tile_pool(name="hid_grouped_pool", bufs=2))
         hid_pool = stack.enter_context(tc.tile_pool(name="hid_pool", bufs=6))
         result_pool = stack.enter_context(tc.tile_pool(name="result_pool", bufs=6))
+        product_pool = stack.enter_context(tc.tile_pool(name="product_pool", bufs=2))
         acc1_pool = stack.enter_context(tc.psum_pool(name="acc1_pool", bufs=4))
         aux_pool = stack.enter_context(tc.psum_pool(name="aux_pool", bufs=4))
 
-        b1_bf16 = consts.tile([P, CHUNKS], BF16)
-        nc.scalar.dma_start(out=b1_bf16[:], in_=eb1.rearrange("(p c) -> p c", c=CHUNKS))
-        b1 = consts.tile([P, CHUNKS], F32)
-        ones = consts.tile([P, P], BF16)
-        nc.vector.memset(ones[:], 1.0)
-        b2_rows = consts.tile([P, WIDTH], BF16)
-        nc.vector.memset(b2_rows[:], 0.0)
-        nc.scalar.dma_start(out=b2_rows[0:1, :], in_=eb2.rearrange("(o n) -> o n", o=1))
-        nc.scalar.activation(out=b1[:], in_=b1_bf16[:], func=IDENTITY)
-        b2_once = consts.tile([P, WIDTH], F32)
-        b2_twice = consts.tile([P, WIDTH], F32)
+        with tc.manual_schedule():
+            b1_bf16 = consts.tile([P, CHUNKS], BF16)
+            nc.scalar.dma_start(out=b1_bf16[:], in_=eb1.rearrange("(p c) -> p c", c=CHUNKS))
+            b1 = consts.tile([P, CHUNKS], F32)
+            ones = consts.tile([P, P], BF16)
+            nc.vector.memset(ones[:], 1.0)
+            b2_rows = consts.tile([P, WIDTH], BF16)
+            nc.vector.memset(b2_rows[:], 0.0)
+            nc.scalar.dma_start(out=b2_rows[0:1, :], in_=eb2.rearrange("(o n) -> o n", o=1))
+            nc.scalar.activation(out=b1[:], in_=b1_bf16[:], func=IDENTITY)
+            b2_once = consts.tile([P, WIDTH], F32)
+            b2_twice = consts.tile([P, WIDTH], F32)
 
-        def spread_b2():
-            b2_spread = aux_pool.tile([P, WIDTH], F32, tag="aux")
-            nc.tensor.matmul(out=b2_spread[:], lhsT=ones[:], rhs=b2_rows[:], start=True, stop=True)
-            nc.vector.tensor_copy(out=b2_once[:], in_=b2_spread[:])
-            nc.vector.tensor_scalar(out=b2_twice[:], in0=b2_spread[:], scalar1=2.0, scalar2=None, op0=MULT)
+            def spread_b2():
+                b2_spread = aux_pool.tile([P, WIDTH], F32, tag="aux")
+                nc.tensor.matmul(out=b2_spread[:], lhsT=ones[:], rhs=b2_rows[:], start=True, stop=True)
+                nc.vector.tensor_copy(out=b2_once[:], in_=b2_spread[:])
+                nc.vector.tensor_scalar(out=b2_twice[:], in0=b2_spread[:], scalar1=2.0, scalar2=None, op0=MULT)
 
-        w1_raw = weights.tile([P, 2, PACK, WIDTH], BF16)
-        for a in range(2):
-            nc.sync.dma_start(
-                out=w1_raw[:, a, :, :],
-                in_=ew1[a * WIDTH : (a + 1) * WIDTH, :].rearrange("(q t) f -> q t f", t=PACK),
-            )
-
-        h_raw = {}
-
-        def load_node_pair(g):
-            for half in range(HALVES):
-                raw = h_raw_pool.tile([P, HALF_TILES * 2 * WIDTH], BF16, name="h_raw", tag="h_raw")
+            w1_raw = weights.tile([P, 2, PACK, WIDTH], BF16)
+            for a in range(2):
                 nc.sync.dma_start(
-                    out=raw[:].rearrange("p (t s k) -> p t s k", t=HALF_TILES, s=2),
-                    in_=h[half * HALF : (half + 1) * HALF, 2 * g : 2 * g + 2, :].rearrange("(t p) s k -> p t s k", p=P),
+                    out=w1_raw[:, a, :, :],
+                    in_=ew1[a * WIDTH : (a + 1) * WIDTH, :].rearrange("(q t) f -> q t f", t=PACK),
                 )
-                h_raw[(g, half)] = raw
 
-        load_node_pair(0)
-        w2_raw = weights.tile([P, PACK, WIDTH], BF16)
-        nc.sync.dma_start(out=w2_raw[:], in_=ew2.rearrange("(p t) n -> p t n", t=PACK))
-        for g in range(1, NODES // 2):
-            load_node_pair(g)
+            h_raw = {}
 
-        ident = consts.tile([P, P], F32)
-        make_identity(nc, ident[:])
-
-        w1_grouped = weights.tile([P, 2, CHUNKS, P, PACK], BF16, align_bytes=64)
-        w1_codes = weights.tile([P, 2, WIDTH], U32, align_bytes=64)
-        w1_scales = weights.tile([P, 2, WIDTH], U8, align_bytes=64)
-        for a in range(2):
-            nc.vector.tensor_copy(
-                out=w1_grouped[:, a, :, :, :],
-                in_=w1_raw[:, a, :, :].rearrange("q t (m c) -> q c m t", c=CHUNKS),
-            )
-        for a in range(2):
-            nc.vector.quantize_mx(
-                out=w1_codes[:, a, :].bitcast(FP8X4),
-                scales=w1_scales[:, a, :],
-                in_=w1_grouped[:, a, :, :, :].rearrange("q c m t -> q (c m t)"),
-            )
-
-        w2_grouped = weights.tile([P, WIDTH, PACK], BF16, align_bytes=64)
-        w2_codes = weights.tile([P, WIDTH], U32, align_bytes=64)
-        w2_scales = weights.tile([P, WIDTH], U8, align_bytes=64)
-
-        def regroup(grouped, planes):
-            nc.vector.tensor_copy(
-                out=grouped[:].rearrange("p (c i) t -> p c t i", i=4),
-                in_=planes[:].rearrange("p t (c i) -> p c t i", i=4),
-            )
-
-        h_codes = nodes.tile([P, NODES, CHAINS], U32, align_bytes=64)
-        h_scales = nodes.tile([P, NODES, CHAINS], U8, align_bytes=64)
-        h_grouped = {}
-
-        def transpose_node(s, half):
-            words = h_raw[(s // 2, half)][:].bitcast(F32)
-            bank = aux_pool.tile([P, 2, HALF], F32, tag="aux")
-            for u in range(2):
-                for t in range(HALF_TILES):
-                    first = (2 * t + s % 2) * WORDS
-                    nc.tensor.transpose(
-                        bank[:, u, t * P : (t + 1) * P], words[:, first + u : first + WORDS : 2], ident[:]
+            def load_node_pair(g):
+                for half in range(HALVES):
+                    raw = h_raw_pool.tile([P, HALF_TILES * 2 * WIDTH], BF16, name="h_raw", tag="h_raw")
+                    nc.sync.dma_start(
+                        out=raw[:].rearrange("p (t s k) -> p t s k", t=HALF_TILES, s=2),
+                        in_=h[half * HALF : (half + 1) * HALF, 2 * g : 2 * g + 2, :].rearrange("(t p) s k -> p t s k", p=P),
                     )
-            grouped = h_grouped_pool.tile([P, HALF * PACK], BF16, name="h_grouped", tag="h_grouped", align_bytes=64)
-            nc.scalar.copy(
-                out=grouped[:].bitcast(F32).rearrange("p (c u) -> p c u", u=2),
-                in_=bank[:].rearrange("p u c -> p c u"),
-            )
-            h_grouped[(s, half)] = grouped
+                    h_raw[(g, half)] = raw
 
-        def quantise_node(s, half):
-            chains = slice(half * HALF, (half + 1) * HALF)
-            nc.vector.quantize_mx(
-                out=h_codes[:, s, chains].bitcast(FP8X4), scales=h_scales[:, s, chains], in_=h_grouped[(s, half)][:]
-            )
+            load_node_pair(0)
+            w2_raw = weights.tile([P, PACK, WIDTH], BF16)
+            nc.sync.dma_start(out=w2_raw[:], in_=ew2.rearrange("(p t) n -> p t n", t=PACK))
+            for g in range(1, NODES // 2):
+                load_node_pair(g)
 
-        planes = {}
-        hid_grouped = {}
-        hid_codes = {}
-        hid_scales = {}
+            ident = consts.tile([P, P], F32)
+            make_identity(nc, ident[:])
 
-        def layer1(i, half):
-            chains = slice(half * HALF, (half + 1) * HALF)
-            hidden = planes_pool.tile([P, CHUNKS, 2, HALF], BF16, name="planes", tag="planes")
-            for c in range(CHUNKS):
-                acc1 = acc1_pool.tile([P, 2, HALF], F32)
-                for direction, joined in ((LR, (i, i + 1)), (RL, (i + 1, i))):
-                    for a in range(2):
-                        nc.tensor.matmul_mx(
-                            out=acc1[:, direction, :],
-                            lhsT=w1_codes[:, a, c * P : (c + 1) * P].bitcast(FP8X4),
-                            lhsT_scale=w1_scales[:, a, c * P : (c + 1) * P],
-                            rhs=h_codes[:, joined[a], chains].bitcast(FP8X4),
-                            rhs_scale=h_scales[:, joined[a], chains],
-                            start=(a == 0),
-                            stop=(a == 1),
-                        )
-                nc.scalar.activation(
-                    out=hidden[:, c, :, :], in_=acc1[:], func=RELU, bias=b1[:, c : c + 1], scale=1.0
+            w1_grouped = weights.tile([P, 2, CHUNKS, P, PACK], BF16, align_bytes=64)
+            w1_codes = weights.tile([P, 2, WIDTH], U32, align_bytes=64)
+            w1_scales = weights.tile([P, 2, WIDTH], U8, align_bytes=64)
+            for a in range(2):
+                for copy, chunks in ((nc.vector.tensor_copy, slice(0, 2)), (nc.scalar.copy, slice(2, CHUNKS))):
+                    copy(
+                        out=w1_grouped[:, a, chunks, :, :],
+                        in_=w1_raw[:, a, :, :].rearrange("q t (m c) -> q c m t", c=CHUNKS)[:, chunks],
+                    )
+            for a in range(2):
+                nc.vector.quantize_mx(
+                    out=w1_codes[:, a, :].bitcast(FP8X4),
+                    scales=w1_scales[:, a, :],
+                    in_=w1_grouped[:, a, :, :, :].rearrange("q c m t -> q (c m t)"),
                 )
-            planes[(i, half)] = hidden
 
-        def regroup_hidden(i, half):
-            grouped = hid_grouped_pool.tile([P, 2 * HALF, PACK], BF16, name="hid_grouped", tag="hid_grouped", align_bytes=64)
-            regroup(grouped, planes[(i, half)][:].rearrange("p t d w -> p t (d w)"))
-            hid_grouped[(i, half)] = grouped
+            w2_grouped = weights.tile([P, WIDTH, PACK], BF16, align_bytes=64)
+            w2_codes = weights.tile([P, WIDTH], U32, align_bytes=64)
+            w2_scales = weights.tile([P, WIDTH], U8, align_bytes=64)
 
-        def quantise_hidden(i, half):
-            codes = hid_pool.tile([P, 2 * HALF], U32, name="hid_codes", tag="hid_codes", align_bytes=64)
-            scales = hid_pool.tile([P, 2 * HALF], U8, name="hid_scales", tag="hid_scales", align_bytes=64)
-            nc.vector.quantize_mx(
-                out=codes[:].bitcast(FP8X4),
-                scales=scales[:],
-                in_=hid_grouped[(i, half)][:].rearrange("p w t -> p (w t)"),
-            )
-            hid_codes[(i, half)] = codes
-            hid_scales[(i, half)] = scales
+            def regroup(copy, grouped, planes):
+                copy(
+                    out=grouped.rearrange("p (c i) t -> p c t i", i=4),
+                    in_=planes.rearrange("p t (c i) -> p c t i", i=4),
+                )
 
-        def layer2(j, half):
-            messages = []
-            if j > 0:
-                messages.append((j - 1, LR))
-            if j < EDGES:
-                messages.append((j, RL))
-            bias = b2_twice if len(messages) == 2 else b2_once
-            for t in range(HALF_TILES):
-                acc2 = aux_pool.tile([P, WIDTH], F32, tag="aux")
+            h_codes = nodes.tile([P, NODES, CHAINS], U32, align_bytes=64)
+            h_scales = nodes.tile([P, NODES, CHAINS], U8, align_bytes=64)
+            h_grouped = {}
+
+            def transpose_node(s, half):
+                words = h_raw[(s // 2, half)][:].bitcast(F32)
+                bank = aux_pool.tile([P, 2, HALF], F32, tag="aux")
+                for u in range(2):
+                    for t in range(HALF_TILES):
+                        first = (2 * t + s % 2) * WORDS
+                        nc.tensor.transpose(
+                            bank[:, u, t * P : (t + 1) * P], words[:, first + u : first + WORDS : 2], ident[:]
+                        )
+                if half == 0:
+                    h_grouped[s] = h_grouped_pool.tile([P, CHAINS * PACK], BF16, name="h_grouped", tag="h_grouped", align_bytes=64)
+                grouped = h_grouped[s][:, half * HALF * PACK : (half + 1) * HALF * PACK]
+                nc.scalar.copy(
+                    out=grouped.bitcast(F32).rearrange("p (c u) -> p c u", u=2),
+                    in_=bank[:].rearrange("p u c -> p c u"),
+                )
+
+            def quantise_node(s, halves=range(HALVES)):
+                chains = slice(halves[0] * HALF, (halves[-1] + 1) * HALF)
+                nc.vector.quantize_mx(
+                    out=h_codes[:, s, chains].bitcast(FP8X4),
+                    scales=h_scales[:, s, chains],
+                    in_=h_grouped[s][:, halves[0] * HALF * PACK : (halves[-1] + 1) * HALF * PACK],
+                )
+
+            planes = {}
+            hid_grouped = {}
+            hid = {}
+
+            def layer1(unit, chunks=range(CHUNKS)):
+                i, half, directions = unit
+                chains = slice(half * HALF, (half + 1) * HALF)
+                n = len(directions) * HALF
+                if chunks[0] == 0:
+                    planes[unit] = planes_pool.tile([P, CHUNKS, n], BF16, name="planes", tag="planes")
+                for c in chunks:
+                    acc1 = acc1_pool.tile([P, n], F32)
+                    for d, direction in enumerate(directions):
+                        joined = (i, i + 1) if direction == LR else (i + 1, i)
+                        for a in range(2):
+                            nc.tensor.matmul_mx(
+                                out=acc1[:, d * HALF : (d + 1) * HALF],
+                                lhsT=w1_codes[:, a, c * P : (c + 1) * P].bitcast(FP8X4),
+                                lhsT_scale=w1_scales[:, a, c * P : (c + 1) * P],
+                                rhs=h_codes[:, joined[a], chains].bitcast(FP8X4),
+                                rhs_scale=h_scales[:, joined[a], chains],
+                                start=(a == 0),
+                                stop=(a == 1),
+                            )
+                    nc.scalar.activation(
+                        out=planes[unit][:, c, :], in_=acc1[:], func=RELU, bias=b1[:, c : c + 1], scale=1.0
+                    )
+
+            def regroup_hidden(unit, share=0):
+                n = len(unit[2]) * HALF
+                grouped = hid_grouped_pool.tile([P, n, PACK], BF16, name="hid_grouped", tag="hid_grouped", align_bytes=64)
+                cut = n - share
+                regroup(nc.vector.tensor_copy, grouped[:, :cut, :], planes[unit][:, :, :cut])
+                if cut < n:
+                    regroup(nc.scalar.copy, grouped[:, cut:, :], planes[unit][:, :, cut:])
+                hid_grouped[unit] = grouped
+
+            def quantise_hidden(unit):
+                i, half, directions = unit
+                n = len(directions) * HALF
+                codes = hid_pool.tile([P, n], U32, name="hid_codes", tag="hid_codes", align_bytes=64)
+                scales = hid_pool.tile([P, n], U8, name="hid_scales", tag="hid_scales", align_bytes=64)
+                nc.vector.quantize_mx(
+                    out=codes[:].bitcast(FP8X4),
+                    scales=scales[:],
+                    in_=hid_grouped[unit][:].rearrange("p w t -> p (w t)"),
+                )
+                for d, direction in enumerate(directions):
+                    for t in range(HALF_TILES):
+                        columns = slice(d * HALF + t * P, d * HALF + (t + 1) * P)
+                        hid[(i, direction, half, t)] = (codes[:, columns], scales[:, columns])
+
+            acc2 = {}
+
+            def layer2(j, half, t):
+                messages = []
+                if j > 0:
+                    messages.append((j - 1, LR))
+                if j < EDGES:
+                    messages.append((j, RL))
+                bank = aux_pool.tile([P, WIDTH], F32, name="acc2", tag="aux")
                 for n, (i, direction) in enumerate(messages):
-                    columns = slice(direction * HALF + t * P, direction * HALF + (t + 1) * P)
+                    codes, scales = hid[(i, direction, half, t)]
                     nc.tensor.matmul_mx(
-                        out=acc2[:],
-                        lhsT=hid_codes[(i, half)][:, columns].bitcast(FP8X4),
-                        lhsT_scale=hid_scales[(i, half)][:, columns],
+                        out=bank[:],
+                        lhsT=codes.bitcast(FP8X4),
+                        lhsT_scale=scales,
                         rhs=w2_codes[:].bitcast(FP8X4),
                         rhs_scale=w2_scales[:],
                         start=(n == 0),
                         stop=(n == len(messages) - 1),
                     )
-                result = result_pool.tile([P, WIDTH], F32)
-                nc.vector.tensor_tensor(out=result[:], in0=acc2[:], in1=bias[:], op=ADD)
+                acc2[(j, half, t)] = bank
+
+            def store(j, half, t, gpsimd=False):
+                bias = b2_twice if 0 < j < EDGES else b2_once
+                result = result_pool.tile([P, WIDTH], F32, name="result", tag="result")
+                if gpsimd:
+                    product = product_pool.tile([P, WIDTH], F32, name="product", tag="product")
+                    nc.scalar.copy(out=product[:], in_=acc2[(j, half, t)][:])
+                    nc.gpsimd.tensor_tensor(out=result[:], in0=product[:], in1=bias[:], op=ADD)
+                else:
+                    nc.vector.tensor_tensor(out=result[:], in0=acc2[(j, half, t)][:], in1=bias[:], op=ADD)
                 first_chain = half * HALF + t * P
                 nc.sync.dma_start(out=out[first_chain : first_chain + P, j, :], in_=result[:])
 
-        for half in range(HALVES):
-            for s in range(2):
-                transpose_node(s, half)
-        for half in range(HALVES):
-            for s in range(2):
-                quantise_node(s, half)
-        regroup(w2_grouped, w2_raw)
+            for half in range(HALVES):
+                for s in range(2):
+                    transpose_node(s, half)
+            for half in range(HALVES):
+                for s in range(2):
+                    quantise_node(s, (half,))
+            regroup(nc.vector.tensor_copy, w2_grouped[:], w2_raw[:])
 
-        def second_layer_after(unit):
-            i, half = unit
-            layer2(i, half)
-            if i == EDGES - 1:
-                layer2(NODES - 1, half)
+            def outputs_of(unit):
+                i, half, directions = unit
+                ends = []
+                if RL in directions:
+                    ends.append(i)
+                if LR in directions and i == EDGES - 1:
+                    ends.append(i + 1)
+                return [(j, half, t) for j in ends for t in range(HALF_TILES)]
 
-        units = [(i, half) for i in range(EDGES) for half in range(HALVES)]
-        for u, (i, half) in enumerate(units):
-            layer1(i, half)
+        stack.enter_context(tc.manual_schedule(engines={mybir.EngineType.PE, mybir.EngineType.SP}))
+        both = (LR, RL)
+        units = [(i, half, both) for i in range(EDGES - 2) for half in range(HALVES)]
+        units += [(5, 0, both), (6, 0, both), (5, 1, both), (6, 1, (RL,)), (6, 1, (LR,))]
+        todo = []
+        next_node = 2
+        for u, unit in enumerate(units):
+            i, half, directions = unit
+            todo.append(outputs_of(unit))
+            layer1(unit)
             if u == 0:
                 spread_b2()
                 nc.vector.quantize_mx(
@@ -231,16 +264,29 @@ def tile_graphnetlayer_pa_t_kernel(tc, h, ew1, eb1, ew2, eb2, out):
                     scales=w2_scales[:],
                     in_=w2_grouped[:].rearrange("p w t -> p (w t)"),
                 )
-            if u >= LAG:
-                second_layer_after(units[u - LAG])
-            new_node = half == 0 and i + 2 < NODES
-            if new_node:
+            lag = 2
+            done = []
+            while len(todo) > lag:
+                done += todo.pop(0)
+            first = done
+            for output in first:
+                layer2(*output)
+                store(*output)
+            new_nodes = []
+            if u + 2 < len(units) and units[u + 2][0] + 1 == next_node:
+                new_nodes.append(next_node)
+                next_node += 1
+            for s in new_nodes:
                 for other in range(HALVES):
-                    transpose_node(i + 2, other)
-            regroup_hidden(i, half)
-            if new_node:
-                for other in range(HALVES):
-                    quantise_node(i + 2, other)
-            quantise_hidden(i, half)
-        for unit in units[len(units) - LAG :]:
-            second_layer_after(unit)
+                    transpose_node(s, other)
+            regroup_hidden(unit, 128 if u > 3 and u % 2 == 1 else 0)
+            for output in done[len(first):]:
+                layer2(*output)
+                store(*output)
+            for s in new_nodes:
+                quantise_node(s)
+            quantise_hidden(unit)
+        for outputs in todo:
+            for output in outputs:
+                layer2(*output)
+                store(*output)

@@ -22,6 +22,7 @@ WORDS = WIDTH // 2
 HALVES = 2
 HALF = CHAINS // HALVES
 HALF_TILES = HALF // P
+LAG = 2
 LR, RL = 0, 1
 
 FLOPS = 2 * 2 * CHAINS * EDGES * (2 * WIDTH * WIDTH + WIDTH * WIDTH)
@@ -35,257 +36,255 @@ def tile_graphnetlayer_pa_t_kernel(tc, h, ew1, eb1, ew2, eb2, out):
         nodes = stack.enter_context(tc.tile_pool(name="nodes", bufs=1))
         h_raw_pool = stack.enter_context(tc.tile_pool(name="h_raw_pool", bufs=HALVES * NODES // 2))
         h_grouped_pool = stack.enter_context(tc.tile_pool(name="h_grouped_pool", bufs=4))
-        planes_pool = stack.enter_context(tc.tile_pool(name="planes_pool", bufs=2))
+        planes_pool = stack.enter_context(tc.tile_pool(name="planes_pool", bufs=3))
         hid_grouped_pool = stack.enter_context(tc.tile_pool(name="hid_grouped_pool", bufs=2))
         hid_pool = stack.enter_context(tc.tile_pool(name="hid_pool", bufs=6))
         result_pool = stack.enter_context(tc.tile_pool(name="result_pool", bufs=6))
-        product_pool = stack.enter_context(tc.tile_pool(name="product_pool", bufs=2))
         acc1_pool = stack.enter_context(tc.psum_pool(name="acc1_pool", bufs=4))
         aux_pool = stack.enter_context(tc.psum_pool(name="aux_pool", bufs=4))
 
-        with tc.manual_schedule():
-            b1_bf16 = consts.tile([P, CHUNKS], BF16)
-            nc.scalar.dma_start(out=b1_bf16[:], in_=eb1.rearrange("(p c) -> p c", c=CHUNKS))
-            b1 = consts.tile([P, CHUNKS], F32)
-            ones = consts.tile([P, P], BF16)
-            nc.vector.memset(ones[:], 1.0)
-            b2_rows = consts.tile([P, WIDTH], BF16)
-            nc.vector.memset(b2_rows[:], 0.0)
-            nc.scalar.dma_start(out=b2_rows[0:1, :], in_=eb2.rearrange("(o n) -> o n", o=1))
-            nc.scalar.activation(out=b1[:], in_=b1_bf16[:], func=IDENTITY)
-            b2_once = consts.tile([P, WIDTH], F32)
-            b2_twice = consts.tile([P, WIDTH], F32)
+        b1_bf16 = consts.tile([P, CHUNKS], BF16)
+        b1 = consts.tile([P, CHUNKS], F32)
+        b2_once = consts.tile([P, WIDTH], BF16)
+        b2_twice = consts.tile([P, WIDTH], BF16)
+        ident = consts.tile([P, P], F32)
+        w1_raw = weights.tile([P, 2, PACK, WIDTH], BF16)
+        w1_grouped = weights.tile([P, CHUNKS, 2, P, PACK], BF16, align_bytes=64)
+        w1_codes = weights.tile([P, CHUNKS, 2, P], U32, align_bytes=64)
+        w1_scales = weights.tile([P, CHUNKS, 2, P], U8, align_bytes=64)
+        w2_raw = weights.tile([P, PACK, WIDTH], BF16)
+        w2_grouped = weights.tile([P, WIDTH, PACK], BF16, align_bytes=64)
+        w2_codes = weights.tile([P, WIDTH], U32, align_bytes=64)
+        w2_scales = weights.tile([P, WIDTH], U8, align_bytes=64)
+        h_codes = nodes.tile([P, NODES, CHAINS], U32, align_bytes=64)
+        h_scales = nodes.tile([P, NODES, CHAINS], U8, align_bytes=64)
+        h_raw = {}
+        h_grouped = {}
+        planes = {}
+        hid_grouped = {}
+        hid = {}
+        acc2 = {}
 
-            def spread_b2():
-                b2_spread = aux_pool.tile([P, WIDTH], F32, tag="aux")
-                nc.tensor.matmul(out=b2_spread[:], lhsT=ones[:], rhs=b2_rows[:], start=True, stop=True)
-                nc.vector.tensor_copy(out=b2_once[:], in_=b2_spread[:])
-                nc.vector.tensor_scalar(out=b2_twice[:], in0=b2_spread[:], scalar1=2.0, scalar2=None, op0=MULT)
+        def load_node_pair(g, half):
+            raw = h_raw_pool.tile([P, HALF_TILES * 2 * WIDTH], BF16, name="h_raw", tag="h_raw")
+            nc.sync.dma_start(
+                out=raw[:].rearrange("p (t s k) -> p t s k", t=HALF_TILES, s=2),
+                in_=h[half * HALF : (half + 1) * HALF, 2 * g : 2 * g + 2, :].rearrange("(t p) s k -> p t s k", p=P),
+            )
+            h_raw[(g, half)] = raw
 
-            w1_raw = weights.tile([P, 2, PACK, WIDTH], BF16)
-            for a in range(2):
-                nc.sync.dma_start(
-                    out=w1_raw[:, a, :, :],
-                    in_=ew1[a * WIDTH : (a + 1) * WIDTH, :].rearrange("(q t) f -> q t f", t=PACK),
+        def load_w1(a):
+            nc.sync.dma_start(
+                out=w1_raw[:, a, :, :],
+                in_=ew1[a * WIDTH : (a + 1) * WIDTH, :].rearrange("(q t) f -> q t f", t=PACK),
+            )
+
+        def regroup_w1(copy, a, c, count=1):
+            copy(
+                out=w1_grouped[:, c : c + count, a, :, :],
+                in_=w1_raw[:, a, :, :].rearrange("q t (m c) -> q c m t", c=CHUNKS)[:, c : c + count],
+            )
+
+        def quantise_w1(c, count=1):
+            nc.vector.quantize_mx(
+                out=w1_codes[:, c : c + count, :, :].rearrange("q c a m -> q (c a m)").bitcast(FP8X4),
+                scales=w1_scales[:, c : c + count, :, :].rearrange("q c a m -> q (c a m)"),
+                in_=w1_grouped[:, c : c + count, :, :, :].rearrange("q c a m t -> q (c a m t)"),
+            )
+
+        def regroup(copy, grouped, planes):
+            copy(
+                out=grouped.rearrange("p (c i) t -> p c t i", i=4),
+                in_=planes.rearrange("p t (c i) -> p c t i", i=4),
+            )
+
+        def quantise_w2():
+            nc.vector.quantize_mx(
+                out=w2_codes[:].bitcast(FP8X4),
+                scales=w2_scales[:],
+                in_=w2_grouped[:].rearrange("p w t -> p (w t)"),
+            )
+
+        def transpose_node(s, half):
+            words = h_raw[(s // 2, half)][:].bitcast(F32)
+            bank = aux_pool.tile([P, 2, HALF], F32, name="h_bank", tag="aux")
+            for u in range(2):
+                for t in range(HALF_TILES):
+                    first = (2 * t + s % 2) * WORDS
+                    nc.tensor.transpose(
+                        bank[:, u, t * P : (t + 1) * P], words[:, first + u : first + WORDS : 2], ident[:]
+                    )
+            if s not in h_grouped:
+                h_grouped[s] = h_grouped_pool.tile([P, CHAINS * PACK], BF16, name="h_grouped", tag="h_grouped", align_bytes=64)
+            grouped = h_grouped[s][:, half * HALF * PACK : (half + 1) * HALF * PACK]
+            nc.scalar.copy(
+                out=grouped.bitcast(F32).rearrange("p (c u) -> p c u", u=2),
+                in_=bank[:].rearrange("p u c -> p c u"),
+            )
+
+        def quantise_node(s, halves=range(HALVES)):
+            chains = slice(halves[0] * HALF, (halves[-1] + 1) * HALF)
+            nc.vector.quantize_mx(
+                out=h_codes[:, s, chains].bitcast(FP8X4),
+                scales=h_scales[:, s, chains],
+                in_=h_grouped[s][:, halves[0] * HALF * PACK : (halves[-1] + 1) * HALF * PACK],
+            )
+
+
+        def layer1(unit, chunks=range(CHUNKS)):
+            i, half, directions = unit
+            chains = slice(half * HALF, (half + 1) * HALF)
+            n = len(directions) * HALF
+            if unit not in planes:
+                planes[unit] = planes_pool.tile([P, CHUNKS, n], BF16, name="planes", tag="planes")
+            for c in chunks:
+                acc1 = acc1_pool.tile([P, n], F32, name="acc1", tag="acc1")
+                for d, direction in enumerate(directions):
+                    joined = (i, i + 1) if direction == LR else (i + 1, i)
+                    for a in range(2):
+                        nc.tensor.matmul_mx(
+                            out=acc1[:, d * HALF : (d + 1) * HALF],
+                            lhsT=w1_codes[:, c, a, :].bitcast(FP8X4),
+                            lhsT_scale=w1_scales[:, c, a, :],
+                            rhs=h_codes[:, joined[a], chains].bitcast(FP8X4),
+                            rhs_scale=h_scales[:, joined[a], chains],
+                            start=(a == 0),
+                            stop=(a == 1),
+                        )
+                nc.scalar.activation(
+                    out=planes[unit][:, c, :], in_=acc1[:], func=RELU, bias=b1[:, c : c + 1], scale=1.0
                 )
 
-            h_raw = {}
+        def regroup_hidden(unit, scalar_share=0):
+            n = len(unit[2]) * HALF
+            grouped = hid_grouped_pool.tile([P, n, PACK], BF16, name="hid_grouped", tag="hid_grouped", align_bytes=64)
+            cut = n - scalar_share
+            regroup(nc.vector.tensor_copy, grouped[:, :cut, :], planes[unit][:, :, :cut])
+            if scalar_share:
+                regroup(nc.scalar.copy, grouped[:, cut:, :], planes[unit][:, :, cut:])
+            hid_grouped[unit] = grouped
 
-            def load_node_pair(g):
-                for half in range(HALVES):
-                    raw = h_raw_pool.tile([P, HALF_TILES * 2 * WIDTH], BF16, name="h_raw", tag="h_raw")
-                    nc.sync.dma_start(
-                        out=raw[:].rearrange("p (t s k) -> p t s k", t=HALF_TILES, s=2),
-                        in_=h[half * HALF : (half + 1) * HALF, 2 * g : 2 * g + 2, :].rearrange("(t p) s k -> p t s k", p=P),
-                    )
-                    h_raw[(g, half)] = raw
+        def quantise_hidden(unit):
+            i, half, directions = unit
+            n = len(directions) * HALF
+            codes = hid_pool.tile([P, n], U32, name="hid_codes", tag="hid_codes", align_bytes=64)
+            scales = hid_pool.tile([P, n], U8, name="hid_scales", tag="hid_scales", align_bytes=64)
+            nc.vector.quantize_mx(
+                out=codes[:].bitcast(FP8X4),
+                scales=scales[:],
+                in_=hid_grouped[unit][:].rearrange("p w t -> p (w t)"),
+            )
+            for d, direction in enumerate(directions):
+                for t in range(HALF_TILES):
+                    columns = slice(d * HALF + t * P, d * HALF + (t + 1) * P)
+                    hid[(i, direction, half, t)] = (codes[:, columns], scales[:, columns])
 
-            load_node_pair(0)
-            w2_raw = weights.tile([P, PACK, WIDTH], BF16)
-            nc.sync.dma_start(out=w2_raw[:], in_=ew2.rearrange("(p t) n -> p t n", t=PACK))
-            for g in range(1, NODES // 2):
-                load_node_pair(g)
+        def outputs_of(unit):
+            i, half, directions = unit
+            ends = []
+            if RL in directions:
+                ends.append(i)
+            if LR in directions and i == EDGES - 1:
+                ends.append(i + 1)
+            return [(j, half, t) for j in ends for t in range(HALF_TILES)]
 
-            ident = consts.tile([P, P], F32)
+        def layer2(j, half, t):
+            messages = []
+            if j > 0:
+                messages.append((j - 1, LR))
+            if j < EDGES:
+                messages.append((j, RL))
+            bank = aux_pool.tile([P, WIDTH], F32, name="acc2", tag="aux")
+            for n, (i, direction) in enumerate(messages):
+                codes, scales = hid[(i, direction, half, t)]
+                nc.tensor.matmul_mx(
+                    out=bank[:],
+                    lhsT=codes.bitcast(FP8X4),
+                    lhsT_scale=scales,
+                    rhs=w2_codes[:].bitcast(FP8X4),
+                    rhs_scale=w2_scales[:],
+                    start=(n == 0),
+                    stop=(n == len(messages) - 1),
+                )
+            acc2[(j, half, t)] = bank
+
+        def store(j, half, t):
+            bias = b2_twice if 0 < j < EDGES else b2_once
+            result = result_pool.tile([P, WIDTH], F32, name="result", tag="result")
+            nc.vector.tensor_tensor(out=result[:], in0=acc2[(j, half, t)][:], in1=bias[:], op=ADD)
+            first_chain = half * HALF + t * P
+            nc.sync.dma_start(out=out[first_chain : first_chain + P, j, :], in_=result[:])
+
+        both = (LR, RL)
+        units = [(i, half, both) for i in range(EDGES - 2) for half in range(HALVES)]
+        units += [(i, 0, both) for i in (EDGES - 2, EDGES - 1)]
+        units += [(EDGES - 2, 1, both), (EDGES - 1, 1, (RL,)), (EDGES - 1, 1, (LR,))]
+
+        with tc.manual_schedule():
+            nc.scalar.dma_start(out=b1_bf16[:], in_=eb1.rearrange("(p c) -> p c", c=CHUNKS))
+            nc.scalar.activation(out=b1[:], in_=b1_bf16[:], func=IDENTITY)
             make_identity(nc, ident[:])
 
-            w1_grouped = weights.tile([P, 2, CHUNKS, P, PACK], BF16, align_bytes=64)
-            w1_codes = weights.tile([P, 2, WIDTH], U32, align_bytes=64)
-            w1_scales = weights.tile([P, 2, WIDTH], U8, align_bytes=64)
-            for a in range(2):
-                for copy, chunks in ((nc.vector.tensor_copy, slice(0, 2)), (nc.scalar.copy, slice(2, CHUNKS))):
-                    copy(
-                        out=w1_grouped[:, a, chunks, :, :],
-                        in_=w1_raw[:, a, :, :].rearrange("q t (m c) -> q c m t", c=CHUNKS)[:, chunks],
-                    )
-            for a in range(2):
-                nc.vector.quantize_mx(
-                    out=w1_codes[:, a, :].bitcast(FP8X4),
-                    scales=w1_scales[:, a, :],
-                    in_=w1_grouped[:, a, :, :, :].rearrange("q c m t -> q (c m t)"),
-                )
+            for part in range(2):
+                load_w1(part)
+                load_node_pair(0, part)
+            for half in range(HALVES):
+                load_node_pair(1, half)
+            nc.sync.dma_start(out=w2_raw[:], in_=ew2.rearrange("(p t) n -> p t n", t=PACK))
+            for g in range(2, NODES // 2):
+                for half in range(HALVES):
+                    load_node_pair(g, half)
+            nc.sync.dma_start(out=b2_once[:], in_=eb2.partition_broadcast(P))
 
-            w2_grouped = weights.tile([P, WIDTH, PACK], BF16, align_bytes=64)
-            w2_codes = weights.tile([P, WIDTH], U32, align_bytes=64)
-            w2_scales = weights.tile([P, WIDTH], U8, align_bytes=64)
-
-            def regroup(copy, grouped, planes):
-                copy(
-                    out=grouped.rearrange("p (c i) t -> p c t i", i=4),
-                    in_=planes.rearrange("p t (c i) -> p c t i", i=4),
-                )
-
-            h_codes = nodes.tile([P, NODES, CHAINS], U32, align_bytes=64)
-            h_scales = nodes.tile([P, NODES, CHAINS], U8, align_bytes=64)
-            h_grouped = {}
-
-            def transpose_node(s, half):
-                words = h_raw[(s // 2, half)][:].bitcast(F32)
-                bank = aux_pool.tile([P, 2, HALF], F32, tag="aux")
-                for u in range(2):
-                    for t in range(HALF_TILES):
-                        first = (2 * t + s % 2) * WORDS
-                        nc.tensor.transpose(
-                            bank[:, u, t * P : (t + 1) * P], words[:, first + u : first + WORDS : 2], ident[:]
-                        )
-                if half == 0:
-                    h_grouped[s] = h_grouped_pool.tile([P, CHAINS * PACK], BF16, name="h_grouped", tag="h_grouped", align_bytes=64)
-                grouped = h_grouped[s][:, half * HALF * PACK : (half + 1) * HALF * PACK]
-                nc.scalar.copy(
-                    out=grouped.bitcast(F32).rearrange("p (c u) -> p c u", u=2),
-                    in_=bank[:].rearrange("p u c -> p c u"),
-                )
-
-            def quantise_node(s, halves=range(HALVES)):
-                chains = slice(halves[0] * HALF, (halves[-1] + 1) * HALF)
-                nc.vector.quantize_mx(
-                    out=h_codes[:, s, chains].bitcast(FP8X4),
-                    scales=h_scales[:, s, chains],
-                    in_=h_grouped[s][:, halves[0] * HALF * PACK : (halves[-1] + 1) * HALF * PACK],
-                )
-
-            planes = {}
-            hid_grouped = {}
-            hid = {}
-
-            def layer1(unit, chunks=range(CHUNKS)):
-                i, half, directions = unit
-                chains = slice(half * HALF, (half + 1) * HALF)
-                n = len(directions) * HALF
-                if chunks[0] == 0:
-                    planes[unit] = planes_pool.tile([P, CHUNKS, n], BF16, name="planes", tag="planes")
-                for c in chunks:
-                    acc1 = acc1_pool.tile([P, n], F32)
-                    for d, direction in enumerate(directions):
-                        joined = (i, i + 1) if direction == LR else (i + 1, i)
-                        for a in range(2):
-                            nc.tensor.matmul_mx(
-                                out=acc1[:, d * HALF : (d + 1) * HALF],
-                                lhsT=w1_codes[:, a, c * P : (c + 1) * P].bitcast(FP8X4),
-                                lhsT_scale=w1_scales[:, a, c * P : (c + 1) * P],
-                                rhs=h_codes[:, joined[a], chains].bitcast(FP8X4),
-                                rhs_scale=h_scales[:, joined[a], chains],
-                                start=(a == 0),
-                                stop=(a == 1),
-                            )
-                    nc.scalar.activation(
-                        out=planes[unit][:, c, :], in_=acc1[:], func=RELU, bias=b1[:, c : c + 1], scale=1.0
-                    )
-
-            def regroup_hidden(unit, share=0):
-                n = len(unit[2]) * HALF
-                grouped = hid_grouped_pool.tile([P, n, PACK], BF16, name="hid_grouped", tag="hid_grouped", align_bytes=64)
-                cut = n - share
-                regroup(nc.vector.tensor_copy, grouped[:, :cut, :], planes[unit][:, :, :cut])
-                if cut < n:
-                    regroup(nc.scalar.copy, grouped[:, cut:, :], planes[unit][:, :, cut:])
-                hid_grouped[unit] = grouped
-
-            def quantise_hidden(unit):
-                i, half, directions = unit
-                n = len(directions) * HALF
-                codes = hid_pool.tile([P, n], U32, name="hid_codes", tag="hid_codes", align_bytes=64)
-                scales = hid_pool.tile([P, n], U8, name="hid_scales", tag="hid_scales", align_bytes=64)
-                nc.vector.quantize_mx(
-                    out=codes[:].bitcast(FP8X4),
-                    scales=scales[:],
-                    in_=hid_grouped[unit][:].rearrange("p w t -> p (w t)"),
-                )
-                for d, direction in enumerate(directions):
-                    for t in range(HALF_TILES):
-                        columns = slice(d * HALF + t * P, d * HALF + (t + 1) * P)
-                        hid[(i, direction, half, t)] = (codes[:, columns], scales[:, columns])
-
-            acc2 = {}
-
-            def layer2(j, half, t):
-                messages = []
-                if j > 0:
-                    messages.append((j - 1, LR))
-                if j < EDGES:
-                    messages.append((j, RL))
-                bank = aux_pool.tile([P, WIDTH], F32, name="acc2", tag="aux")
-                for n, (i, direction) in enumerate(messages):
-                    codes, scales = hid[(i, direction, half, t)]
-                    nc.tensor.matmul_mx(
-                        out=bank[:],
-                        lhsT=codes.bitcast(FP8X4),
-                        lhsT_scale=scales,
-                        rhs=w2_codes[:].bitcast(FP8X4),
-                        rhs_scale=w2_scales[:],
-                        start=(n == 0),
-                        stop=(n == len(messages) - 1),
-                    )
-                acc2[(j, half, t)] = bank
-
-            def store(j, half, t, gpsimd=False):
-                bias = b2_twice if 0 < j < EDGES else b2_once
-                result = result_pool.tile([P, WIDTH], F32, name="result", tag="result")
-                if gpsimd:
-                    product = product_pool.tile([P, WIDTH], F32, name="product", tag="product")
-                    nc.scalar.copy(out=product[:], in_=acc2[(j, half, t)][:])
-                    nc.gpsimd.tensor_tensor(out=result[:], in0=product[:], in1=bias[:], op=ADD)
-                else:
-                    nc.vector.tensor_tensor(out=result[:], in0=acc2[(j, half, t)][:], in1=bias[:], op=ADD)
-                first_chain = half * HALF + t * P
-                nc.sync.dma_start(out=out[first_chain : first_chain + P, j, :], in_=result[:])
-
+            regroup_w1(nc.vector.tensor_copy, 0, 0, 2)
+            regroup_w1(nc.scalar.copy, 0, 2, 2)
             for half in range(HALVES):
                 for s in range(2):
                     transpose_node(s, half)
-            for half in range(HALVES):
-                for s in range(2):
-                    quantise_node(s, (half,))
+                if half == 0:
+                    regroup_w1(nc.scalar.copy, 1, 2, 2)
+            regroup_w1(nc.vector.tensor_copy, 1, 0, 2)
+            quantise_w1(0)
+            for s in range(2):
+                quantise_node(s, (0,))
+            quantise_w1(1)
+            quantise_w1(2, 2)
+            for s in range(2):
+                quantise_node(s, (1,))
             regroup(nc.vector.tensor_copy, w2_grouped[:], w2_raw[:])
 
-            def outputs_of(unit):
-                i, half, directions = unit
-                ends = []
-                if RL in directions:
-                    ends.append(i)
-                if LR in directions and i == EDGES - 1:
-                    ends.append(i + 1)
-                return [(j, half, t) for j in ends for t in range(HALF_TILES)]
-
         stack.enter_context(tc.manual_schedule(engines={mybir.EngineType.PE, mybir.EngineType.SP}))
-        both = (LR, RL)
-        units = [(i, half, both) for i in range(EDGES - 2) for half in range(HALVES)]
-        units += [(5, 0, both), (6, 0, both), (5, 1, both), (6, 1, (RL,)), (6, 1, (LR,))]
         todo = []
         next_node = 2
         for u, unit in enumerate(units):
-            i, half, directions = unit
             todo.append(outputs_of(unit))
             layer1(unit)
             if u == 0:
-                spread_b2()
-                nc.vector.quantize_mx(
-                    out=w2_codes[:].bitcast(FP8X4),
-                    scales=w2_scales[:],
-                    in_=w2_grouped[:].rearrange("p w t -> p (w t)"),
+                quantise_w2()
+                nc.gpsimd.tensor_scalar(
+                    out=b2_twice[:], in0=b2_once[:], scalar1=2.0, scalar2=0.0, op0=MULT, op1=ADD
                 )
-            lag = 2
-            done = []
-            while len(todo) > lag:
-                done += todo.pop(0)
-            first = done
-            for output in first:
-                layer2(*output)
-                store(*output)
+            hidden_first = u >= len(units) - 4
+            if hidden_first:
+                regroup_hidden(unit, HALF // 2)
+                quantise_hidden(unit)
+            while len(todo) > LAG:
+                for output in todo.pop(0):
+                    layer2(*output)
+                    store(*output)
             new_nodes = []
             if u + 2 < len(units) and units[u + 2][0] + 1 == next_node:
                 new_nodes.append(next_node)
                 next_node += 1
             for s in new_nodes:
-                for other in range(HALVES):
-                    transpose_node(s, other)
-            regroup_hidden(unit, 128 if u > 3 and u % 2 == 1 else 0)
-            for output in done[len(first):]:
-                layer2(*output)
-                store(*output)
+                for half in range(HALVES):
+                    transpose_node(s, half)
+            if not hidden_first:
+                regroup_hidden(unit, HALF // 2 if u > 3 and u % 2 == 1 else 0)
             for s in new_nodes:
                 quantise_node(s)
-            quantise_hidden(unit)
+            if not hidden_first:
+                quantise_hidden(unit)
         for outputs in todo:
             for output in outputs:
                 layer2(*output)

@@ -50,14 +50,14 @@ def tile_graphnetlayer_pa_t_kernel(tc, h, ew1, eb1, ew2, eb2, out):
         ident = consts.tile([P, P], F32)
         w1_raw = weights.tile([P, 2, PACK, WIDTH], BF16)
         w1_grouped = weights.tile([P, CHUNKS, 2, P, PACK], BF16, align_bytes=64)
-        w1_codes = weights.tile([P, CHUNKS, 2, P], U32, align_bytes=64)
-        w1_scales = weights.tile([P, CHUNKS, 2, P], U8, align_bytes=64)
+        w1_codes = weights.tile([P, CHUNKS, 2, P], U32, align_bytes=256)
+        w1_scales = weights.tile([P, CHUNKS, 2, P], U8, align_bytes=256)
         w2_raw = weights.tile([P, PACK, WIDTH], BF16)
         w2_grouped = weights.tile([P, WIDTH, PACK], BF16, align_bytes=64)
-        w2_codes = weights.tile([P, WIDTH], U32, align_bytes=64)
-        w2_scales = weights.tile([P, WIDTH], U8, align_bytes=64)
-        h_codes = nodes.tile([P, NODES, CHAINS], U32, align_bytes=64)
-        h_scales = nodes.tile([P, NODES, CHAINS], U8, align_bytes=64)
+        w2_codes = weights.tile([P, WIDTH], U32, align_bytes=256)
+        w2_scales = weights.tile([P, WIDTH], U8, align_bytes=256)
+        h_codes = nodes.tile([P, NODES, CHAINS], U32, align_bytes=256)
+        h_scales = nodes.tile([P, NODES, CHAINS], U8, align_bytes=256)
         h_raw = {}
         h_grouped = {}
         planes = {}
@@ -167,8 +167,8 @@ def tile_graphnetlayer_pa_t_kernel(tc, h, ew1, eb1, ew2, eb2, out):
         def quantise_hidden(unit):
             i, half, directions = unit
             n = len(directions) * HALF
-            codes = hid_pool.tile([P, n], U32, name="hid_codes", tag="hid_codes", align_bytes=64)
-            scales = hid_pool.tile([P, n], U8, name="hid_scales", tag="hid_scales", align_bytes=64)
+            codes = hid_pool.tile([P, n], U32, name="hid_codes", tag="hid_codes", align_bytes=256)
+            scales = hid_pool.tile([P, n], U8, name="hid_scales", tag="hid_scales", align_bytes=256)
             nc.vector.quantize_mx(
                 out=codes[:].bitcast(FP8X4),
                 scales=scales[:],

from contextlib import ExitStack

import concourse.mybir as mybir
from concourse.masks import make_identity

BF16 = mybir.dt.bfloat16
F32 = mybir.dt.float32
U32 = mybir.dt.uint32
U8 = mybir.dt.uint8
FP8X4 = mybir.dt.float8_e4m3fn_x4
RELU = mybir.ActivationFunctionType.Relu
IDENTITY = mybir.ActivationFunctionType.Identity
ADD = mybir.AluOpType.add
MULT = mybir.AluOpType.mult

P = 128
PACK = 4
CHAINS, NODES, WIDTH = 512, 8, 512
EDGES = NODES - 1
CHUNKS = WIDTH // P
WORDS = WIDTH // 2
HALVES = 2
HALF = CHAINS // HALVES
HALF_TILES = HALF // P
LAG = 2
LR, RL = 0, 1

FLOPS = 2 * 2 * CHAINS * EDGES * (2 * WIDTH * WIDTH + WIDTH * WIDTH)


def tile_graphnetlayer_pa_t_kernel(tc, h, ew1, eb1, ew2, eb2, out):
    nc = tc.nc
    with ExitStack() as stack:
        consts = stack.enter_context(tc.tile_pool(name="consts", bufs=1))
        weights = stack.enter_context(tc.tile_pool(name="weights", bufs=1))
        nodes = stack.enter_context(tc.tile_pool(name="nodes", bufs=1))
        h_raw_pool = stack.enter_context(tc.tile_pool(name="h_raw_pool", bufs=HALVES * NODES // 2))
        h_grouped_pool = stack.enter_context(tc.tile_pool(name="h_grouped_pool", bufs=4))
        planes_pool = stack.enter_context(tc.tile_pool(name="planes_pool", bufs=3))
        hid_grouped_pool = stack.enter_context(tc.tile_pool(name="hid_grouped_pool", bufs=2))
        hid_pool = stack.enter_context(tc.tile_pool(name="hid_pool", bufs=6))
        result_pool = stack.enter_context(tc.tile_pool(name="result_pool", bufs=6))
        acc1_pool = stack.enter_context(tc.psum_pool(name="acc1_pool", bufs=4))
        aux_pool = stack.enter_context(tc.psum_pool(name="aux_pool", bufs=4))

        b1_bf16 = consts.tile([P, CHUNKS], BF16)
        b1 = consts.tile([P, CHUNKS], F32)
        b2_once = consts.tile([P, WIDTH], BF16)
        b2_twice = consts.tile([P, WIDTH], BF16)
        ident = consts.tile([P, P], F32)
        w1_raw = weights.tile([P, 2, PACK, WIDTH], BF16)
        w1_grouped = weights.tile([P, CHUNKS, 2, P, PACK], BF16, align_bytes=64)
        w1_codes = weights.tile([P, CHUNKS, 2, P], U32, align_bytes=256)
        w1_scales = weights.tile([P, CHUNKS, 2, P], U8, align_bytes=256)
        w2_raw = weights.tile([P, PACK, WIDTH], BF16)
        w2_grouped = weights.tile([P, WIDTH, PACK], BF16, align_bytes=64)
        w2_codes = weights.tile([P, WIDTH], U32, align_bytes=256)
        w2_scales = weights.tile([P, WIDTH], U8, align_bytes=256)
        h_codes = nodes.tile([P, NODES, CHAINS], U32, align_bytes=256)
        h_scales = nodes.tile([P, NODES, CHAINS], U8, align_bytes=256)
        h_raw = {}
        h_grouped = {}
        planes = {}
        hid_grouped = {}
        hid = {}
        acc2 = {}

        def load_node_pair(g, half):
            raw = h_raw_pool.tile([P, HALF_TILES * 2 * WIDTH], BF16, name="h_raw", tag="h_raw")
            nc.sync.dma_start(
                out=raw[:].rearrange("p (t s k) -> p t s k", t=HALF_TILES, s=2),
                in_=h[half * HALF : (half + 1) * HALF, 2 * g : 2 * g + 2, :].rearrange("(t p) s k -> p t s k", p=P),
            )
            h_raw[(g, half)] = raw

        def load_w1(a):
            nc.sync.dma_start(
                out=w1_raw[:, a, :, :],
                in_=ew1[a * WIDTH : (a + 1) * WIDTH, :].rearrange("(q t) f -> q t f", t=PACK),
            )

        def regroup_w1(copy, a, c, count=1):
            copy(
                out=w1_grouped[:, c : c + count, a, :, :],
                in_=w1_raw[:, a, :, :].rearrange("q t (m c) -> q c m t", c=CHUNKS)[:, c : c + count],
            )

        def quantise_w1(c, count=1):
            nc.vector.quantize_mx(
                out=w1_codes[:, c : c + count, :, :].rearrange("q c a m -> q (c a m)").bitcast(FP8X4),
                scales=w1_scales[:, c : c + count, :, :].rearrange("q c a m -> q (c a m)"),
                in_=w1_grouped[:, c : c + count, :, :, :].rearrange("q c a m t -> q (c a m t)"),
            )

        def regroup(copy, grouped, planes):
            copy(
                out=grouped.rearrange("p (c i) t -> p c t i", i=4),
                in_=planes.rearrange("p t (c i) -> p c t i", i=4),
            )

        def quantise_w2():
            nc.vector.quantize_mx(
                out=w2_codes[:].bitcast(FP8X4),
                scales=w2_scales[:],
                in_=w2_grouped[:].rearrange("p w t -> p (w t)"),
            )

        def transpose_node(s, half):
            words = h_raw[(s // 2, half)][:].bitcast(F32)
            bank = aux_pool.tile([P, 2, HALF], F32, name="h_bank", tag="aux")
            for u in range(2):
                for t in range(HALF_TILES):
                    first = (2 * t + s % 2) * WORDS
                    nc.tensor.transpose(
                        bank[:, u, t * P : (t + 1) * P], words[:, first + u : first + WORDS : 2], ident[:]
                    )
            if s not in h_grouped:
                h_grouped[s] = h_grouped_pool.tile([P, CHAINS * PACK], BF16, name="h_grouped", tag="h_grouped", align_bytes=64)
            grouped = h_grouped[s][:, half * HALF * PACK : (half + 1) * HALF * PACK]
            nc.scalar.copy(
                out=grouped.bitcast(F32).rearrange("p (c u) -> p c u", u=2),
                in_=bank[:].rearrange("p u c -> p c u"),
            )

        def quantise_node(s, halves=range(HALVES)):
            chains = slice(halves[0] * HALF, (halves[-1] + 1) * HALF)
            nc.vector.quantize_mx(
                out=h_codes[:, s, chains].bitcast(FP8X4),
                scales=h_scales[:, s, chains],
                in_=h_grouped[s][:, halves[0] * HALF * PACK : (halves[-1] + 1) * HALF * PACK],
            )


        def layer1(unit, chunks=range(CHUNKS)):
            i, half, directions = unit
            chains = slice(half * HALF, (half + 1) * HALF)
            n = len(directions) * HALF
            if unit not in planes:
                planes[unit] = planes_pool.tile([P, CHUNKS, n], BF16, name="planes", tag="planes")
            for c in chunks:
                acc1 = acc1_pool.tile([P, n], F32, name="acc1", tag="acc1")
                for d, direction in enumerate(directions):
                    joined = (i, i + 1) if direction == LR else (i + 1, i)
                    for a in range(2):
                        nc.tensor.matmul_mx(
                            out=acc1[:, d * HALF : (d + 1) * HALF],
                            lhsT=w1_codes[:, c, a, :].bitcast(FP8X4),
                            lhsT_scale=w1_scales[:, c, a, :],
                            rhs=h_codes[:, joined[a], chains].bitcast(FP8X4),
                            rhs_scale=h_scales[:, joined[a], chains],
                            start=(a == 0),
                            stop=(a == 1),
                        )
                nc.scalar.activation(
                    out=planes[unit][:, c, :], in_=acc1[:], func=RELU, bias=b1[:, c : c + 1], scale=1.0
                )

        def regroup_hidden(unit, scalar_share=0):
            n = len(unit[2]) * HALF
            grouped = hid_grouped_pool.tile([P, n, PACK], BF16, name="hid_grouped", tag="hid_grouped", align_bytes=64)
            cut = n - scalar_share
            regroup(nc.vector.tensor_copy, grouped[:, :cut, :], planes[unit][:, :, :cut])
            if scalar_share:
                regroup(nc.scalar.copy, grouped[:, cut:, :], planes[unit][:, :, cut:])
            hid_grouped[unit] = grouped

        def quantise_hidden(unit):
            i, half, directions = unit
            n = len(directions) * HALF
            codes = hid_pool.tile([P, n], U32, name="hid_codes", tag="hid_codes", align_bytes=256)
            scales = hid_pool.tile([P, n], U8, name="hid_scales", tag="hid_scales", align_bytes=256)
            nc.vector.quantize_mx(
                out=codes[:].bitcast(FP8X4),
                scales=scales[:],
                in_=hid_grouped[unit][:].rearrange("p w t -> p (w t)"),
            )
            for d, direction in enumerate(directions):
                for t in range(HALF_TILES):
                    columns = slice(d * HALF + t * P, d * HALF + (t + 1) * P)
                    hid[(i, direction, half, t)] = (codes[:, columns], scales[:, columns])

        def outputs_of(unit):
            i, half, directions = unit
            ends = []
            if RL in directions:
                ends.append(i)
            if LR in directions and i == EDGES - 1:
                ends.append(i + 1)
            return [(j, half, t) for j in ends for t in range(HALF_TILES)]

        def layer2(j, half, t):
            messages = []
            if j > 0:
                messages.append((j - 1, LR))
            if j < EDGES:
                messages.append((j, RL))
            bank = aux_pool.tile([P, WIDTH], F32, name="acc2", tag="aux")
            for n, (i, direction) in enumerate(messages):
                codes, scales = hid[(i, direction, half, t)]
                nc.tensor.matmul_mx(
                    out=bank[:],
                    lhsT=codes.bitcast(FP8X4),
                    lhsT_scale=scales,
                    rhs=w2_codes[:].bitcast(FP8X4),
                    rhs_scale=w2_scales[:],
                    start=(n == 0),
                    stop=(n == len(messages) - 1),
                )
            acc2[(j, half, t)] = bank

        def store(j, half, t):
            bias = b2_twice if 0 < j < EDGES else b2_once
            result = result_pool.tile([P, WIDTH], F32, name="result", tag="result")
            nc.vector.tensor_tensor(out=result[:], in0=acc2[(j, half, t)][:], in1=bias[:], op=ADD)
            first_chain = half * HALF + t * P
            nc.sync.dma_start(out=out[first_chain : first_chain + P, j, :], in_=result[:])

        both = (LR, RL)
        units = [(i, half, both) for i in range(EDGES - 2) for half in range(HALVES)]
        units += [(i, 0, both) for i in (EDGES - 2, EDGES - 1)]
        units += [(EDGES - 2, 1, both), (EDGES - 1, 1, (RL,)), (EDGES - 1, 1, (LR,))]

        with tc.manual_schedule():
            nc.scalar.dma_start(out=b1_bf16[:], in_=eb1.rearrange("(p c) -> p c", c=CHUNKS))
            nc.scalar.activation(out=b1[:], in_=b1_bf16[:], func=IDENTITY)
            make_identity(nc, ident[:])

            for part in range(2):
                load_w1(part)
                load_node_pair(0, part)
            for half in range(HALVES):
                load_node_pair(1, half)
            nc.sync.dma_start(out=w2_raw[:], in_=ew2.rearrange("(p t) n -> p t n", t=PACK))
            for g in range(2, NODES // 2):
                for half in range(HALVES):
                    load_node_pair(g, half)
            nc.sync.dma_start(out=b2_once[:], in_=eb2.partition_broadcast(P))

            regroup_w1(nc.vector.tensor_copy, 0, 0, 2)
            regroup_w1(nc.scalar.copy, 0, 2, 2)
            for half in range(HALVES):
                for s in range(2):
                    transpose_node(s, half)
                if half == 0:
                    regroup_w1(nc.scalar.copy, 1, 2, 2)
            regroup_w1(nc.vector.tensor_copy, 1, 0, 2)
            quantise_w1(0)
            for s in range(2):
                quantise_node(s, (0,))
            quantise_w1(1)
            quantise_w1(2, 2)
            for s in range(2):
                quantise_node(s, (1,))
            regroup(nc.vector.tensor_copy, w2_grouped[:], w2_raw[:])

        stack.enter_context(tc.manual_schedule(engines={mybir.EngineType.PE, mybir.EngineType.SP}))
        todo = []
        next_node = 2
        for u, unit in enumerate(units):
            todo.append(outputs_of(unit))
            layer1(unit)
            if u == 0:
                quantise_w2()
                nc.gpsimd.tensor_scalar(
                    out=b2_twice[:], in0=b2_once[:], scalar1=2.0, scalar2=0.0, op0=MULT, op1=ADD
                )
            hidden_first = u >= len(units) - 4
            if hidden_first:
                regroup_hidden(unit, HALF // 2)
                quantise_hidden(unit)
            while len(todo) > LAG:
                for output in todo.pop(0):
                    layer2(*output)
                    store(*output)
            new_nodes = []
            if u + 2 < len(units) and units[u + 2][0] + 1 == next_node:
                new_nodes.append(next_node)
                next_node += 1
            for s in new_nodes:
                for half in range(HALVES):
                    transpose_node(s, half)
            if not hidden_first:
                regroup_hidden(unit, HALF // 2 if u > 3 and u % 2 == 1 else 0)
            for s in new_nodes:
                quantise_node(s)
            if not hidden_first:
                quantise_hidden(unit)
        for outputs in todo:
            for output in outputs:
                layer2(*output)
                store(*output)
